import numpy as np
import ml_dtypes


def mxq(x, axis, fmt="e4m3"):
    dtype, down = {"e4m3": (ml_dtypes.float8_e4m3fn, 7), "e5m2": (ml_dtypes.float8_e5m2, 14)}[fmt]
    v = np.moveaxis(np.asarray(x, np.float32).astype(ml_dtypes.bfloat16).astype(np.float64), axis, -1)
    blocks = v.reshape(v.shape[:-1] + (-1, 32))
    amax = np.abs(blocks).max(-1, keepdims=True)
    byte = np.maximum(np.where(amax > 0, np.frexp(amax)[1] - 1 + 127, 0) - down, 1)
    scale = np.exp2(byte - 127.0)
    codes = (blocks / scale).astype(np.float32).astype(dtype).astype(np.float64)
    return np.moveaxis((codes * scale).reshape(v.shape), -1, axis)


WIDE = False


def mx_kscale(k):
    if not WIDE:
        return np.ones(k)
    levels = np.array([10, -10, 5, -5, 0])
    a = np.random.permutation(np.resize(levels, k // 512 * 4)).reshape(k // 512, 4)
    idx = np.arange(k)
    return np.exp2(a[idx // 512, idx % 128 // 32])


BF16 = ml_dtypes.bfloat16


def bf(x):
    return np.asarray(x, np.float32).astype(BF16)


def f64(x):
    return np.asarray(x).astype(np.float64)


B, H, W, FI, FO = 2, 64, 64, 1024, 128

OFFSETS = [(-1, 0), (1, 0), (0, -1), (0, 1), (-1, -1), (-1, 1), (1, -1), (1, 1)]


def setup_inputs():
    s = mx_kscale(FI)
    return {"X": bf(np.random.standard_normal((B, H * W, FI)) * 0.5 * s),
            "Wm": bf(np.random.standard_normal((FI, FO)) / np.sqrt(FI) / s[:, None]),
            "b": bf(np.random.standard_normal(FO) * 0.2),
            "H": H, "W": W}


def reference(X, Wm, b, H, W):
    X = f64(X)
    Bn, N, F = X.shape
    Xg = X.reshape(Bn, H, W, F)
    P = np.pad(Xg, ((0, 0), (1, 1), (1, 1), (0, 0)))
    AX = P[:, 1 + OFFSETS[0][0]:1 + OFFSETS[0][0] + H,
           1 + OFFSETS[0][1]:1 + OFFSETS[0][1] + W, :]
    for dr, dc in OFFSETS[1:]:
        AX = AX + P[:, 1 + dr:1 + dr + H, 1 + dc:1 + dc + W, :]
    AX = AX.reshape(Bn, N, F)
    return (mxq(AX, 2, "e4m3") @ mxq(f64(Wm), 0, "e4m3")) + f64(b)

@@ -1,0 +1,159 @@
+from contextlib import ExitStack
+
+import concourse.mybir as mybir
+from concourse.masks import make_identity
+
+F32 = mybir.dt.float32
+BF16 = mybir.dt.bfloat16
+U32 = mybir.dt.uint32
+U8 = mybir.dt.uint8
+FP8X4 = mybir.dt.float8_e4m3fn_x4
+ADD = mybir.AluOpType.add
+
+P = 128
+IMAGES, GH, GW, FI, FO = 2, 64, 64, 1024, 128
+PACK = 4
+PASSES = FI // (P * PACK)
+CW = 2
+CAST_EVERY, CAST_PHASE = 6, 3
+FLOPS = 2 * IMAGES * GH * GW * FI * FO + 7 * IMAGES * GH * GW * FI
+
+
+def tile_graphconvlayer_t_kernel(tc, X, Wm, b, H, W, out):
+    nc = tc.nc
+    assert (H, W) == (GH, GW)
+    x_view = X.rearrange("i (r c) f -> (i r) c f", c=GW)
+    out_view = out.rearrange("i (r c) o -> (i r) c o", c=GW)
+
+    with ExitStack() as ctx:
+        const = ctx.enter_context(tc.tile_pool(name="const", bufs=1))
+        sums = ctx.enter_context(tc.tile_pool(name="sums", bufs=3))
+        masked = ctx.enter_context(tc.tile_pool(name="masked", bufs=2))
+        quant = ctx.enter_context(tc.tile_pool(name="quant", bufs=3))
+        outs = ctx.enter_context(tc.tile_pool(name="outs", bufs=4))
+        psum_ax = ctx.enter_context(tc.psum_pool(name="psum_ax", bufs=6))
+        psum_o = ctx.enter_context(tc.psum_pool(name="psum_o", bufs=2))
+
+        xs = const.tile([P, GW + 2, FI], BF16, name="xs")
+        nc.vector.memset(xs[:, 0, :], 0.0)
+        nc.vector.memset(xs[:, GW + 1, :], 0.0)
+        cuts = [0, 3, 4] + list(range(8, GW + 1, 4))
+        for lo, hi in zip(cuts[:-1], cuts[1:]):
+            nc.sync.dma_start(out=xs[:, 1 + lo : 1 + hi, :], in_=x_view[:, lo:hi, :])
+
+        wraw = const.tile([P, PASSES * PACK, FO], BF16, name="wraw")
+        nc.scalar.dma_start(out=wraw[:], in_=Wm.rearrange("(a p) n -> p a n", p=P))
+        braw = const.tile([P, FO], BF16, name="braw")
+        nc.scalar.dma_start(out=braw[:], in_=b.partition_broadcast(P))
+
+        ident = const.tile([P, P], F32, name="ident")
+        make_identity(nc, ident[:])
+        pair_a = const.tile([P, P], F32, name="pair_a")
+        pair_b = const.tile([P, P], F32, name="pair_b")
+        pair_c = const.tile([P, P], F32, name="pair_c")
+
+        def halves(ap):
+            view = ap.rearrange("p (j two) -> p j two", two=2)
+            return view[:, :, 0], view[:, :, 1]
+
+        a_even, a_odd = halves(pair_a[:])
+        i_even, i_odd = halves(ident[:])
+        nc.vector.tensor_copy(out=a_even, in_=i_odd)
+        nc.vector.tensor_copy(out=a_odd, in_=i_even)
+        nc.vector.memset(pair_b[:], 0.0)
+        for i in range(IMAGES):
+            inner = slice(i * GH + 1, i * GH + GH - 1)
+            b_first, b_second = halves(pair_b[:, inner])
+            i_first, i_second = halves(ident[:, inner])
+            nc.vector.tensor_copy(out=b_first, in_=i_second)
+            nc.vector.tensor_copy(out=b_second, in_=i_first)
+        inner_rows = const.tile([P, 1], F32, name="inner_rows")
+        nc.vector.reduce_sum(out=inner_rows[:], in_=pair_b[:], axis=mybir.AxisListType.X)
+        nc.vector.tensor_copy(out=pair_c[:], in_=pair_b[:])
+        for i in range(IMAGES):
+            top, bottom = i * GH, i * GH + GH - 1
+            nc.vector.tensor_copy(out=pair_c[:, top : top + 1], in_=ident[:, bottom : bottom + 1])
+            nc.vector.tensor_copy(out=pair_c[:, bottom : bottom + 1], in_=ident[:, top : top + 1])
+
+        wcodes = const.tile([P, PASSES, FO], U32, name="wcodes", align_bytes=64)
+        wscale = const.tile([P, PASSES, FO], U8, name="wscale", align_bytes=64)
+        bias32 = const.tile([P, FO], F32, name="bias32")
+
+        def prepare_weights():
+            wgrp = const.tile([P, PASSES, FO, PACK], BF16, name="wgrp", align_bytes=64)
+            nc.vector.tensor_copy(
+                out=wgrp[:],
+                in_=wraw[:].rearrange("p (g t) n -> p g n t", t=PACK),
+            )
+            nc.vector.tensor_copy(out=bias32[:], in_=braw[:])
+            nc.vector.quantize_mx(
+                out=wcodes[:].rearrange("p g n -> p (g n)").bitcast(FP8X4),
+                scales=wscale[:].rearrange("p g n -> p (g n)"),
+                in_=wgrp[:].rearrange("p g n t -> p (g n t)"),
+            )
+
+        def flat(ap):
+            return ap.rearrange("p c f -> p (c f)")
+
+        for k in range(GW // CW):
+            c0 = k * CW
+            tt = sums.tile([P, CW, FI], F32, name="tt")
+            ss = sums.tile([P, CW, FI], F32, name="ss")
+            nc.vector.tensor_tensor(
+                out=flat(tt[:]), in0=flat(xs[:, c0 : c0 + CW, :]), in1=flat(xs[:, c0 + 2 : c0 + 2 + CW, :]), op=ADD
+            )
+            centre = flat(xs[:, c0 + 1 : c0 + 1 + CW, :])
+            if k % CAST_EVERY == CAST_PHASE:
+                sm = masked.tile([P, CW, FI], F32, name="sm")
+                nc.scalar.copy(out=flat(ss[:]), in_=centre)
+                nc.scalar.activation(
+                    out=flat(sm[:]), in_=centre, func=mybir.ActivationFunctionType.Copy, scale=inner_rows[:, 0:1]
+                )
+                terms = [(tt, pair_b), (tt, ident), (tt, pair_a), (ss, pair_a), (sm, pair_c)]
+            else:
+                nc.vector.tensor_tensor(out=flat(ss[:]), in0=flat(tt[:]), in1=centre, op=ADD)
+                terms = [(ss, pair_b), (tt, ident), (ss, pair_a)]
+            if k == 0:
+                prepare_weights()
+
+            grouped = quant.tile([P, CW, PASSES, P, PACK], BF16, name="grouped", align_bytes=64)
+            for cc in range(CW):
+                for g in range(PASSES):
+                    ax = psum_ax.tile([P, PACK, P], F32, name="ax")
+                    for t in range(PACK):
+                        cols = slice((g * PACK + t) * P, (g * PACK + t + 1) * P)
+                        for j, (data, matrix) in enumerate(terms):
+                            nc.tensor.matmul(
+                                out=ax[:, t, :], lhsT=data[:, cc, cols], rhs=matrix[:],
+                                is_transpose=True, start=(j == 0), stop=(j == len(terms) - 1),
+                            )
+                    nc.scalar.copy(out=grouped[:, cc, g], in_=ax[:].rearrange("p t n -> p n t"))
+
+            codes = quant.tile([P, CW, PASSES, P], U32, name="codes", align_bytes=64)
+            scales = quant.tile([P, CW, PASSES, P], U8, name="scales", align_bytes=64)
+            nc.vector.quantize_mx(
+                out=codes[:].rearrange("p c g n -> p (c g n)").bitcast(FP8X4),
+                scales=scales[:].rearrange("p c g n -> p (c g n)"),
+                in_=grouped[:].rearrange("p c g n t -> p (c g n t)"),
+            )
+
+            po = psum_o.tile([P, CW, FO], F32, name="po")
+            for cc in range(CW):
+                for g in range(PASSES):
+                    nc.tensor.matmul_mx(
+                        out=po[:, cc, :],
+                        lhsT=codes[:, cc, g, :].bitcast(FP8X4),
+                        lhsT_scale=scales[:, cc, g, :],
+                        rhs=wcodes[:, g, :].bitcast(FP8X4),
+                        rhs_scale=wscale[:, g, :],
+                        start=(g == 0),
+                        stop=(g == PASSES - 1),
+                    )
+            osb = outs.tile([P, CW, FO], F32, name="osb")
+            nc.vector.tensor_tensor(
+                out=osb[:],
+                in0=po[:],
+                in1=bias32[:].unsqueeze(1).to_broadcast([P, CW, FO]),
+                op=ADD,
+            )
+            nc.sync.dma_start(out=out_view[:, c0 : c0 + CW, :], in_=osb[:])

@@ -15,7 +15,10 @@ IMAGES, GH, GW, FI, FO = 2, 64, 64, 1024, 128
 PACK = 4
 PASSES = FI // (P * PACK)
 CW = 2
-CAST_EVERY, CAST_PHASE = 6, 3
+NCH = GW // CW
+NPAD = 512
+LAG_T, LAG_Q, LAG_M, LAG_B = 1, 3, 4, 6
+FIRST_KICK, KICK, KICK_EVERY = 10, 3, 4
 FLOPS = 2 * IMAGES * GH * GW * FI * FO + 7 * IMAGES * GH * GW * FI
 
 
@@ -28,132 +31,167 @@ def tile_graphconvlayer_t_kernel(tc, X, Wm, b, H, W, out):
     with ExitStack() as ctx:
         const = ctx.enter_context(tc.tile_pool(name="const", bufs=1))
         sums = ctx.enter_context(tc.tile_pool(name="sums", bufs=3))
-        masked = ctx.enter_context(tc.tile_pool(name="masked", bufs=2))
         quant = ctx.enter_context(tc.tile_pool(name="quant", bufs=3))
         outs = ctx.enter_context(tc.tile_pool(name="outs", bufs=4))
-        psum_ax = ctx.enter_context(tc.psum_pool(name="psum_ax", bufs=6))
-        psum_o = ctx.enter_context(tc.psum_pool(name="psum_o", bufs=2))
+        psum_ax = ctx.enter_context(tc.psum_pool(name="psum_ax", bufs=4))
+        psum_o = ctx.enter_context(tc.psum_pool(name="psum_o", bufs=3))
+        psum_j = ctx.enter_context(tc.psum_pool(name="psum_j", bufs=1))
+        ctx.enter_context(tc.manual_schedule())
+
+        def flat(ap):
+            return ap.rearrange("p c f -> p (c f)")
 
         xs = const.tile([P, GW + 2, FI], BF16, name="xs")
-        nc.vector.memset(xs[:, 0, :], 0.0)
-        nc.vector.memset(xs[:, GW + 1, :], 0.0)
-        cuts = [0, 3, 4] + list(range(8, GW + 1, 4))
+        cuts = [0, 2, 4] + list(range(8, GW + 1, 4))
         for lo, hi in zip(cuts[:-1], cuts[1:]):
             nc.sync.dma_start(out=xs[:, 1 + lo : 1 + hi, :], in_=x_view[:, lo:hi, :])
-
         wraw = const.tile([P, PASSES * PACK, FO], BF16, name="wraw")
         nc.scalar.dma_start(out=wraw[:], in_=Wm.rearrange("(a p) n -> p a n", p=P))
         braw = const.tile([P, FO], BF16, name="braw")
         nc.scalar.dma_start(out=braw[:], in_=b.partition_broadcast(P))
 
+        fill = const.tile([P, NPAD * PACK], BF16, name="fill", align_bytes=64)
+        nc.vector.memset(fill[:], 1.0)
+        dq = const.tile([P, NPAD], U32, name="dq", align_bytes=64)
+        dqs = const.tile([P, NPAD], U8, name="dqs", align_bytes=64)
+        nc.vector.quantize_mx(out=dq[:].bitcast(FP8X4), scales=dqs[:], in_=fill[:])
+        junk = psum_j.tile([P, NPAD], F32, name="junk")
+
+        def filler_pass():
+            nc.tensor.matmul_mx(
+                out=junk[:], lhsT=dq[:, 0:P].bitcast(FP8X4), lhsT_scale=dqs[:, 0:P],
+                rhs=dq[:].bitcast(FP8X4), rhs_scale=dqs[:], start=True, stop=True,
+            )
+
         ident = const.tile([P, P], F32, name="ident")
         make_identity(nc, ident[:])
         pair_a = const.tile([P, P], F32, name="pair_a")
         pair_b = const.tile([P, P], F32, name="pair_b")
-        pair_c = const.tile([P, P], F32, name="pair_c")
 
         def halves(ap):
             view = ap.rearrange("p (j two) -> p j two", two=2)
             return view[:, :, 0], view[:, :, 1]
 
+        nc.vector.memset(pair_b[:], 0.0)
+        nc.vector.memset(xs[:, 0, :], 0.0)
+        nc.vector.memset(xs[:, GW + 1, :], 0.0)
         a_even, a_odd = halves(pair_a[:])
         i_even, i_odd = halves(ident[:])
         nc.vector.tensor_copy(out=a_even, in_=i_odd)
         nc.vector.tensor_copy(out=a_odd, in_=i_even)
-        nc.vector.memset(pair_b[:], 0.0)
         for i in range(IMAGES):
             inner = slice(i * GH + 1, i * GH + GH - 1)
             b_first, b_second = halves(pair_b[:, inner])
             i_first, i_second = halves(ident[:, inner])
             nc.vector.tensor_copy(out=b_first, in_=i_second)
             nc.vector.tensor_copy(out=b_second, in_=i_first)
-        inner_rows = const.tile([P, 1], F32, name="inner_rows")
-        nc.vector.reduce_sum(out=inner_rows[:], in_=pair_b[:], axis=mybir.AxisListType.X)
-        nc.vector.tensor_copy(out=pair_c[:], in_=pair_b[:])
-        for i in range(IMAGES):
-            top, bottom = i * GH, i * GH + GH - 1
-            nc.vector.tensor_copy(out=pair_c[:, top : top + 1], in_=ident[:, bottom : bottom + 1])
-            nc.vector.tensor_copy(out=pair_c[:, bottom : bottom + 1], in_=ident[:, top : top + 1])
 
-        wcodes = const.tile([P, PASSES, FO], U32, name="wcodes", align_bytes=64)
-        wscale = const.tile([P, PASSES, FO], U8, name="wscale", align_bytes=64)
+        wq = const.tile([P, PASSES, NPAD], U32, name="wq", align_bytes=64)
+        wqs = const.tile([P, PASSES, NPAD], U8, name="wqs", align_bytes=64)
+        for g in range(PASSES):
+            nc.vector.quantize_mx(out=wq[:, g, :].bitcast(FP8X4), scales=wqs[:, g, :], in_=fill[:])
         bias32 = const.tile([P, FO], F32, name="bias32")
 
         def prepare_weights():
             wgrp = const.tile([P, PASSES, FO, PACK], BF16, name="wgrp", align_bytes=64)
-            nc.vector.tensor_copy(
-                out=wgrp[:],
-                in_=wraw[:].rearrange("p (g t) n -> p g n t", t=PACK),
-            )
+            nc.vector.tensor_copy(out=wgrp[:], in_=wraw[:].rearrange("p (g t) n -> p g n t", t=PACK))
             nc.vector.tensor_copy(out=bias32[:], in_=braw[:])
-            nc.vector.quantize_mx(
-                out=wcodes[:].rearrange("p g n -> p (g n)").bitcast(FP8X4),
-                scales=wscale[:].rearrange("p g n -> p (g n)"),
-                in_=wgrp[:].rearrange("p g n t -> p (g n t)"),
-            )
+            for g in range(PASSES):
+                nc.vector.quantize_mx(
+                    out=wq[:, g, 0:FO].bitcast(FP8X4),
+                    scales=wqs[:, g, 0:FO],
+                    in_=wgrp[:, g].rearrange("p n t -> p (n t)"),
+                )
 
-        def flat(ap):
-            return ap.rearrange("p c f -> p (c f)")
+        sums_of, grouped_of, codes_of, staged_of, po_of = {}, {}, {}, {}, {}
 
-        for k in range(GW // CW):
-            c0 = k * CW
+        def column_sums(k):
             tt = sums.tile([P, CW, FI], F32, name="tt")
             ss = sums.tile([P, CW, FI], F32, name="ss")
-            nc.vector.tensor_tensor(
-                out=flat(tt[:]), in0=flat(xs[:, c0 : c0 + CW, :]), in1=flat(xs[:, c0 + 2 : c0 + 2 + CW, :]), op=ADD
-            )
-            centre = flat(xs[:, c0 + 1 : c0 + 1 + CW, :])
-            if k % CAST_EVERY == CAST_PHASE:
-                sm = masked.tile([P, CW, FI], F32, name="sm")
-                nc.scalar.copy(out=flat(ss[:]), in_=centre)
-                nc.scalar.activation(
-                    out=flat(sm[:]), in_=centre, func=mybir.ActivationFunctionType.Copy, scale=inner_rows[:, 0:1]
+            sums_of[k] = (tt, ss)
+            c0 = k * CW
+            for lo, hi in ([(0, 1), (1, 2)] if k == 0 else [(0, CW)]):
+                nc.vector.tensor_tensor(
+                    out=flat(tt[:, lo:hi, :]), in0=flat(xs[:, c0 + lo : c0 + hi, :]),
+                    in1=flat(xs[:, c0 + lo + 2 : c0 + hi + 2, :]), op=ADD,
                 )
-                terms = [(tt, pair_b), (tt, ident), (tt, pair_a), (ss, pair_a), (sm, pair_c)]
-            else:
-                nc.vector.tensor_tensor(out=flat(ss[:]), in0=flat(tt[:]), in1=centre, op=ADD)
-                terms = [(ss, pair_b), (tt, ident), (ss, pair_a)]
-            if k == 0:
-                prepare_weights()
+                nc.vector.tensor_tensor(
+                    out=flat(ss[:, lo:hi, :]), in0=flat(tt[:, lo:hi, :]),
+                    in1=flat(xs[:, c0 + lo + 1 : c0 + hi + 1, :]), op=ADD,
+                )
 
-            grouped = quant.tile([P, CW, PASSES, P, PACK], BF16, name="grouped", align_bytes=64)
-            for cc in range(CW):
-                for g in range(PASSES):
-                    ax = psum_ax.tile([P, PACK, P], F32, name="ax")
-                    for t in range(PACK):
-                        cols = slice((g * PACK + t) * P, (g * PACK + t + 1) * P)
-                        for j, (data, matrix) in enumerate(terms):
-                            nc.tensor.matmul(
-                                out=ax[:, t, :], lhsT=data[:, cc, cols], rhs=matrix[:],
-                                is_transpose=True, start=(j == 0), stop=(j == len(terms) - 1),
-                            )
-                    nc.scalar.copy(out=grouped[:, cc, g], in_=ax[:].rearrange("p t n -> p n t"))
+        def row_sums(k, cc, g):
+            tt, ss = sums_of[k]
+            if (cc, g) == (0, 0):
+                grouped_of[k] = quant.tile([P, CW, PASSES, P, PACK], BF16, name="grouped", align_bytes=64)
+            ax = psum_ax.tile([P, PACK, P], F32, name="ax")
+            terms = ((ss, pair_b), (tt, ident), (ss, pair_a))
+            for t in range(PACK):
+                cols = slice((g * PACK + t) * P, (g * PACK + t + 1) * P)
+                for j, (data, matrix) in enumerate(terms):
+                    nc.tensor.matmul(
+                        out=ax[:, t, :], lhsT=data[:, cc, cols], rhs=matrix[:],
+                        is_transpose=True, start=(j == 0), stop=(j == len(terms) - 1),
+                    )
+            nc.scalar.copy(out=grouped_of[k][:, cc, g], in_=ax[:].rearrange("p t n -> p n t"))
 
+        def quantise(k):
             codes = quant.tile([P, CW, PASSES, P], U32, name="codes", align_bytes=64)
             scales = quant.tile([P, CW, PASSES, P], U8, name="scales", align_bytes=64)
+            codes_of[k] = (codes, scales)
             nc.vector.quantize_mx(
                 out=codes[:].rearrange("p c g n -> p (c g n)").bitcast(FP8X4),
                 scales=scales[:].rearrange("p c g n -> p (c g n)"),
-                in_=grouped[:].rearrange("p c g n t -> p (c g n t)"),
+                in_=grouped_of[k][:].rearrange("p c g n t -> p (c g n t)"),
             )
 
-            po = psum_o.tile([P, CW, FO], F32, name="po")
-            for cc in range(CW):
-                for g in range(PASSES):
-                    nc.tensor.matmul_mx(
-                        out=po[:, cc, :],
-                        lhsT=codes[:, cc, g, :].bitcast(FP8X4),
-                        lhsT_scale=scales[:, cc, g, :],
-                        rhs=wcodes[:, g, :].bitcast(FP8X4),
-                        rhs_scale=wscale[:, g, :],
-                        start=(g == 0),
-                        stop=(g == PASSES - 1),
-                    )
-            osb = outs.tile([P, CW, FO], F32, name="osb")
-            nc.vector.tensor_tensor(
-                out=osb[:],
-                in0=po[:],
-                in1=bias32[:].unsqueeze(1).to_broadcast([P, CW, FO]),
-                op=ADD,
+        def mx_pass(k, cc, g, width):
+            codes, scales = codes_of[k]
+            if (cc, g) == (0, 0):
+                staged_of[k] = outs.tile([P, CW, FO], F32, name="staged")
+            if g == 0:
+                po_of[k] = psum_o.tile([P, NPAD], F32, name="po")
+            po = po_of[k]
+            nc.tensor.matmul_mx(
+                out=po[:, 0:width],
+                lhsT=codes[:, cc, g, :].bitcast(FP8X4),
+                lhsT_scale=scales[:, cc, g, :],
+                rhs=wq[:, g, 0:width].bitcast(FP8X4),
+                rhs_scale=wqs[:, g, 0:width],
+                start=(g == 0),
+                stop=(g == PASSES - 1),
             )
-            nc.sync.dma_start(out=out_view[:, c0 : c0 + CW, :], in_=osb[:])
+            if g == PASSES - 1:
+                nc.scalar.copy(out=staged_of[k][:, cc, :], in_=po[:, 0:FO])
+
+        def finish(k):
+            staged = staged_of[k]
+            nc.vector.tensor_tensor(
+                out=staged[:], in0=staged[:], in1=bias32[:].unsqueeze(1).to_broadcast([P, CW, FO]), op=ADD
+            )
+            nc.sync.dma_start(out=out_view[:, k * CW : (k + 1) * CW, :], in_=staged[:])
+
+        for n in range(FIRST_KICK):
+            filler_pass()
+
+        for j in range(NCH + LAG_B):
+            if j < NCH:
+                column_sums(j)
+            if j == 2:
+                prepare_weights()
+            if 0 <= j - LAG_Q < NCH:
+                quantise(j - LAG_Q)
+            if 0 <= j - LAG_B < NCH:
+                finish(j - LAG_B)
+            kt, km = j - LAG_T, j - LAG_M
+            for u in range(CW * PASSES):
+                cc, g = divmod(u, PASSES)
+                if 0 <= kt < NCH:
+                    row_sums(kt, cc, g)
+                    if km < 0:
+                        filler_pass()
+                if 0 <= km < NCH:
+                    mx_pass(km, cc, g, NPAD if 0 <= kt < NCH else FO)
+                if u == 0 and 0 <= kt < NCH and j % KICK_EVERY == 1:
+                    for n in range(KICK):
+                        filler_pass()

@@ -18,7 +18,7 @@ CW = 2
 NCH = GW // CW
 NPAD = 512
 LAG_T, LAG_Q, LAG_M, LAG_B = 1, 3, 4, 6
-FIRST_KICK, KICK, KICK_EVERY = 10, 3, 4
+FIRST_KICK = 10
 FLOPS = 2 * IMAGES * GH * GW * FI * FO + 7 * IMAGES * GH * GW * FI
 
 
@@ -184,14 +184,12 @@ def tile_graphconvlayer_t_kernel(tc, X, Wm, b, H, W, out):
             if 0 <= j - LAG_B < NCH:
                 finish(j - LAG_B)
             kt, km = j - LAG_T, j - LAG_M
-            for u in range(CW * PASSES):
-                cc, g = divmod(u, PASSES)
-                if 0 <= kt < NCH:
-                    row_sums(kt, cc, g)
-                    if km < 0:
-                        filler_pass()
-                if 0 <= km < NCH:
-                    mx_pass(km, cc, g, NPAD if 0 <= kt < NCH else FO)
-                if u == 0 and 0 <= kt < NCH and j % KICK_EVERY == 1:
-                    for n in range(KICK):
+            for cc in range(CW):
+                for g in range(PASSES):
+                    if 0 <= kt < NCH:
+                        row_sums(kt, cc, g)
+                for g in range(PASSES):
+                    if 0 <= km < NCH:
+                        mx_pass(km, cc, g, NPAD if 0 <= kt < NCH else FO)
+                    elif km < 0 <= kt:
                         filler_pass()

@@ -14,9 +14,13 @@ P = 128
 IMAGES, GH, GW, FI, FO = 2, 64, 64, 1024, 128
 PACK = 4
 PASSES = FI // (P * PACK)
-CW = 2
-NCH = GW // CW
+HALF = GW // 2
+PAIRS = GH // 2
+BLOCKS = P // PAIRS
+NCH = HALF
 NPAD = 512
+NY = 2
+KB = 2
 LAG_T, LAG_Q, LAG_M, LAG_B = 1, 3, 4, 6
 FIRST_KICK = 10
 FLOPS = 2 * IMAGES * GH * GW * FI * FO + 7 * IMAGES * GH * GW * FI
@@ -25,71 +29,69 @@ FLOPS = 2 * IMAGES * GH * GW * FI * FO + 7 * IMAGES * GH * GW * FI
 def tile_graphconvlayer_t_kernel(tc, X, Wm, b, H, W, out):
     nc = tc.nc
     assert (H, W) == (GH, GW)
-    x_view = X.rearrange("i (r c) f -> (i r) c f", c=GW)
-    out_view = out.rearrange("i (r c) o -> (i r) c o", c=GW)
+    x_views = [X[i].rearrange("(a e c) f -> a e c f", e=2, c=GW) for i in range(IMAGES)]
+    out_views = [out[i].rearrange("(a e c) o -> a e c o", e=2, c=GW) for i in range(IMAGES)]
 
     with ExitStack() as ctx:
         const = ctx.enter_context(tc.tile_pool(name="const", bufs=1))
         sums = ctx.enter_context(tc.tile_pool(name="sums", bufs=3))
         quant = ctx.enter_context(tc.tile_pool(name="quant", bufs=3))
-        outs = ctx.enter_context(tc.tile_pool(name="outs", bufs=4))
+        group = ctx.enter_context(tc.tile_pool(name="group", bufs=3))
+        outs = ctx.enter_context(tc.tile_pool(name="outs", bufs=3))
         psum_ax = ctx.enter_context(tc.psum_pool(name="psum_ax", bufs=4))
         psum_o = ctx.enter_context(tc.psum_pool(name="psum_o", bufs=3))
         psum_j = ctx.enter_context(tc.psum_pool(name="psum_j", bufs=1))
         ctx.enter_context(tc.manual_schedule())
 
-        def flat(ap):
-            return ap.rearrange("p c f -> p (c f)")
+        def block(q):
+            return slice(q * PAIRS, (q + 1) * PAIRS)
 
-        xs = const.tile([P, GW + 2, FI], BF16, name="xs")
-        cuts = [0, 2, 4] + list(range(8, GW + 1, 4))
+        xs = const.tile([P, HALF + 2, 2, FI], BF16, name="xs")
+        cuts = [0, 3, 6] + list(range(10, HALF + 3, 4))
         for lo, hi in zip(cuts[:-1], cuts[1:]):
-            nc.sync.dma_start(out=xs[:, 1 + lo : 1 + hi, :], in_=x_view[:, lo:hi, :])
+            for q in (0, 2, 1, 3):
+                i, h = divmod(q, 2)
+                a, z = max(lo, 1 - h), min(hi, HALF + 2 - h)
+                first = HALF * h - 1
+                for e in range(2):
+                    nc.sync.dma_start(out=xs[block(q), a:z, e, :], in_=x_views[i][:, e, first + a : first + z, :])
         wraw = const.tile([P, PASSES * PACK, FO], BF16, name="wraw")
         nc.scalar.dma_start(out=wraw[:], in_=Wm.rearrange("(a p) n -> p a n", p=P))
         braw = const.tile([P, FO], BF16, name="braw")
         nc.scalar.dma_start(out=braw[:], in_=b.partition_broadcast(P))
 
-        fill = const.tile([P, NPAD * PACK], BF16, name="fill", align_bytes=64)
+        fill = const.tile([P, FO * PACK], BF16, name="fill", align_bytes=64)
         nc.vector.memset(fill[:], 1.0)
-        dq = const.tile([P, NPAD], U32, name="dq", align_bytes=64)
-        dqs = const.tile([P, NPAD], U8, name="dqs", align_bytes=64)
-        nc.vector.quantize_mx(out=dq[:].bitcast(FP8X4), scales=dqs[:], in_=fill[:])
+        wq = const.tile([P, PASSES, NPAD], U32, name="wq", align_bytes=64)
+        wqs = const.tile([P, PASSES, NPAD], U8, name="wqs", align_bytes=64)
+        for g in reversed(range(PASSES)):
+            for lo in range(0, NPAD, FO):
+                nc.vector.quantize_mx(
+                    out=wq[:, g, lo : lo + FO].bitcast(FP8X4), scales=wqs[:, g, lo : lo + FO], in_=fill[:]
+                )
         junk = psum_j.tile([P, NPAD], F32, name="junk")
 
         def filler_pass():
             nc.tensor.matmul_mx(
-                out=junk[:], lhsT=dq[:, 0:P].bitcast(FP8X4), lhsT_scale=dqs[:, 0:P],
-                rhs=dq[:].bitcast(FP8X4), rhs_scale=dqs[:], start=True, stop=True,
+                out=junk[:], lhsT=wq[:, 1, NPAD - P : NPAD].bitcast(FP8X4), lhsT_scale=wqs[:, 1, NPAD - P : NPAD],
+                rhs=wq[:, 1, :].bitcast(FP8X4), rhs_scale=wqs[:, 1, :], start=True, stop=True,
             )
 
         ident = const.tile([P, P], F32, name="ident")
         make_identity(nc, ident[:])
-        pair_a = const.tile([P, P], F32, name="pair_a")
-        pair_b = const.tile([P, P], F32, name="pair_b")
+        above = const.tile([P, P], F32, name="above")
+        below = const.tile([P, P], F32, name="below")
 
-        def halves(ap):
-            view = ap.rearrange("p (j two) -> p j two", two=2)
-            return view[:, :, 0], view[:, :, 1]
+        def blocks(ap):
+            return ap.rearrange("p (q a) -> p q a", q=BLOCKS)
 
-        nc.vector.memset(pair_b[:], 0.0)
-        nc.vector.memset(xs[:, 0, :], 0.0)
-        nc.vector.memset(xs[:, GW + 1, :], 0.0)
-        a_even, a_odd = halves(pair_a[:])
-        i_even, i_odd = halves(ident[:])
-        nc.vector.tensor_copy(out=a_even, in_=i_odd)
-        nc.vector.tensor_copy(out=a_odd, in_=i_even)
-        for i in range(IMAGES):
-            inner = slice(i * GH + 1, i * GH + GH - 1)
-            b_first, b_second = halves(pair_b[:, inner])
-            i_first, i_second = halves(ident[:, inner])
-            nc.vector.tensor_copy(out=b_first, in_=i_second)
-            nc.vector.tensor_copy(out=b_second, in_=i_first)
-
-        wq = const.tile([P, PASSES, NPAD], U32, name="wq", align_bytes=64)
-        wqs = const.tile([P, PASSES, NPAD], U8, name="wqs", align_bytes=64)
-        for g in range(PASSES):
-            nc.vector.quantize_mx(out=wq[:, g, :].bitcast(FP8X4), scales=wqs[:, g, :], in_=fill[:])
+        nc.vector.memset(above[:], 0.0)
+        nc.vector.memset(below[:], 0.0)
+        for q in range(BLOCKS):
+            nc.vector.memset(xs[block(q), (HALF + 1) * (q % 2), :, :], 0.0)
+        nc.vector.tensor_copy(out=blocks(above[:])[:, :, 1:PAIRS], in_=blocks(ident[:])[:, :, 0 : PAIRS - 1])
+        nc.vector.tensor_copy(out=blocks(below[:])[:, :, 0 : PAIRS - 1], in_=blocks(ident[:])[:, :, 1:PAIRS])
+        shift = (above, below)
         bias32 = const.tile([P, FO], F32, name="bias32")
 
         def prepare_weights():
@@ -106,38 +108,58 @@ def tile_graphconvlayer_t_kernel(tc, X, Wm, b, H, W, out):
         sums_of, grouped_of, codes_of, staged_of, po_of = {}, {}, {}, {}, {}
 
         def column_sums(k):
-            tt = sums.tile([P, CW, FI], F32, name="tt")
-            ss = sums.tile([P, CW, FI], F32, name="ss")
-            sums_of[k] = (tt, ss)
-            c0 = k * CW
-            for lo, hi in ([(0, 1), (1, 2)] if k == 0 else [(0, CW)]):
+            tt = sums.tile([P, 2, FI], F32, name="tt")
+            ss = sums.tile([P, 2, FI], F32, name="ss")
+            yy = sums.tile([P, 2, NY * P], F32, name="yy")
+            sums_of[k] = (tt, ss, yy)
+
+            def sides(rows):
+                nc.vector.tensor_tensor(out=tt[:, rows, :], in0=xs[:, k, rows, :], in1=xs[:, k + 2, rows, :], op=ADD)
+
+            def triple(rows):
+                nc.vector.tensor_tensor(out=ss[:, rows, :], in0=tt[:, rows, :], in1=xs[:, k + 1, rows, :], op=ADD)
+
+            def in_pair(e):
                 nc.vector.tensor_tensor(
-                    out=flat(tt[:, lo:hi, :]), in0=flat(xs[:, c0 + lo : c0 + hi, :]),
-                    in1=flat(xs[:, c0 + lo + 2 : c0 + hi + 2, :]), op=ADD,
-                )
-                nc.vector.tensor_tensor(
-                    out=flat(ss[:, lo:hi, :]), in0=flat(tt[:, lo:hi, :]),
-                    in1=flat(xs[:, c0 + lo + 1 : c0 + hi + 1, :]), op=ADD,
+                    out=yy[:, e, :], in0=tt[:, e, 0 : NY * P], in1=ss[:, 1 - e, 0 : NY * P], op=ADD
                 )
 
-        def row_sums(k, cc, g):
-            tt, ss = sums_of[k]
-            if (cc, g) == (0, 0):
-                grouped_of[k] = quant.tile([P, CW, PASSES, P, PACK], BF16, name="grouped", align_bytes=64)
+            if k == 0:
+                sides(slice(1, 2))
+                triple(slice(1, 2))
+                sides(slice(0, 1))
+                in_pair(0)
+                triple(slice(0, 1))
+                in_pair(1)
+            else:
+                sides(slice(0, 2))
+                triple(slice(0, 2))
+                in_pair(0)
+                in_pair(1)
+
+        def row_sums(k, e, g):
+            tt, ss, yy = sums_of[k]
+            if (e, g) == (0, 0):
+                grouped_of[k] = group.tile([P, 2, PASSES, P, PACK], BF16, name="grouped", align_bytes=64)
             ax = psum_ax.tile([P, PACK, P], F32, name="ax")
-            terms = ((ss, pair_b), (tt, ident), (ss, pair_a))
             for t in range(PACK):
-                cols = slice((g * PACK + t) * P, (g * PACK + t + 1) * P)
+                tile_no = g * PACK + t
+                cols = slice(tile_no * P, (tile_no + 1) * P)
+                terms = [(ss[:, 1 - e, cols], shift[e])]
+                if tile_no < NY:
+                    terms += [(yy[:, e, cols], ident)]
+                else:
+                    terms += [(tt[:, e, cols], ident), (ss[:, 1 - e, cols], ident)]
                 for j, (data, matrix) in enumerate(terms):
                     nc.tensor.matmul(
-                        out=ax[:, t, :], lhsT=data[:, cc, cols], rhs=matrix[:],
+                        out=ax[:, t, :], lhsT=data, rhs=matrix[:],
                         is_transpose=True, start=(j == 0), stop=(j == len(terms) - 1),
                     )
-            nc.scalar.copy(out=grouped_of[k][:, cc, g], in_=ax[:].rearrange("p t n -> p n t"))
+            nc.scalar.copy(out=grouped_of[k][:, e, g], in_=ax[:].rearrange("p t n -> p n t"))
 
         def quantise(k):
-            codes = quant.tile([P, CW, PASSES, P], U32, name="codes", align_bytes=64)
-            scales = quant.tile([P, CW, PASSES, P], U8, name="scales", align_bytes=64)
+            codes = quant.tile([P, 2, PASSES, P], U32, name="codes", align_bytes=64)
+            scales = quant.tile([P, 2, PASSES, P], U8, name="scales", align_bytes=64)
             codes_of[k] = (codes, scales)
             nc.vector.quantize_mx(
                 out=codes[:].rearrange("p c g n -> p (c g n)").bitcast(FP8X4),
@@ -145,31 +167,35 @@ def tile_graphconvlayer_t_kernel(tc, X, Wm, b, H, W, out):
                 in_=grouped_of[k][:].rearrange("p c g n t -> p (c g n t)"),
             )
 
-        def mx_pass(k, cc, g, width):
+        def mx_pass(k, e, g, width):
             codes, scales = codes_of[k]
-            if (cc, g) == (0, 0):
-                staged_of[k] = outs.tile([P, CW, FO], F32, name="staged")
+            if (k % KB, e, g) == (0, 0, 0):
+                staged_of[k // KB] = outs.tile([P, 2, KB, FO], F32, name="staged")
             if g == 0:
                 po_of[k] = psum_o.tile([P, NPAD], F32, name="po")
             po = po_of[k]
             nc.tensor.matmul_mx(
                 out=po[:, 0:width],
-                lhsT=codes[:, cc, g, :].bitcast(FP8X4),
-                lhsT_scale=scales[:, cc, g, :],
+                lhsT=codes[:, e, g, :].bitcast(FP8X4),
+                lhsT_scale=scales[:, e, g, :],
                 rhs=wq[:, g, 0:width].bitcast(FP8X4),
                 rhs_scale=wqs[:, g, 0:width],
                 start=(g == 0),
                 stop=(g == PASSES - 1),
             )
             if g == PASSES - 1:
-                nc.scalar.copy(out=staged_of[k][:, cc, :], in_=po[:, 0:FO])
+                nc.scalar.copy(out=staged_of[k // KB][:, e, k % KB, :], in_=po[:, 0:FO])
 
-        def finish(k):
-            staged = staged_of[k]
+        def finish(batch):
+            staged = staged_of[batch]
+            rows = staged[:].rearrange("p e k o -> p (e k) o")
             nc.vector.tensor_tensor(
-                out=staged[:], in0=staged[:], in1=bias32[:].unsqueeze(1).to_broadcast([P, CW, FO]), op=ADD
+                out=rows, in0=rows, in1=bias32[:].unsqueeze(1).to_broadcast([P, 2 * KB, FO]), op=ADD
             )
-            nc.sync.dma_start(out=out_view[:, k * CW : (k + 1) * CW, :], in_=staged[:])
+            for q in range(BLOCKS):
+                i, h = divmod(q, 2)
+                first = HALF * h + batch * KB
+                nc.sync.dma_start(out=out_views[i][:, :, first : first + KB, :], in_=staged[block(q)])
 
         for n in range(FIRST_KICK):
             filler_pass()
@@ -181,15 +207,15 @@ def tile_graphconvlayer_t_kernel(tc, X, Wm, b, H, W, out):
                 prepare_weights()
             if 0 <= j - LAG_Q < NCH:
                 quantise(j - LAG_Q)
-            if 0 <= j - LAG_B < NCH:
-                finish(j - LAG_B)
+            if 0 <= j - LAG_B < NCH and (j - LAG_B) % KB == KB - 1:
+                finish((j - LAG_B) // KB)
             kt, km = j - LAG_T, j - LAG_M
-            for cc in range(CW):
+            for e in range(2):
                 for g in range(PASSES):
                     if 0 <= kt < NCH:
-                        row_sums(kt, cc, g)
+                        row_sums(kt, e, g)
                 for g in range(PASSES):
                     if 0 <= km < NCH:
-                        mx_pass(km, cc, g, NPAD if 0 <= kt < NCH else FO)
+                        mx_pass(km, e, g, NPAD if 0 <= kt < NCH else FO)
                     elif km < 0 <= kt:
                         filler_pass()

@@ -14,84 +14,88 @@ P = 128
 IMAGES, GH, GW, FI, FO = 2, 64, 64, 1024, 128
 PACK = 4
 PASSES = FI // (P * PACK)
-HALF = GW // 2
-PAIRS = GH // 2
-BLOCKS = P // PAIRS
-NCH = HALF
+CW = 2
+NCH = GW // CW
 NPAD = 512
-NY = 2
-KB = 2
-LAG_T, LAG_Q, LAG_M, LAG_B = 1, 3, 4, 6
-FIRST_KICK = 10
+LAG_T, LAG_Q, LAG_M = 1, 3, 4
+FIRST_KICK = 4
+RUN = 7
 FLOPS = 2 * IMAGES * GH * GW * FI * FO + 7 * IMAGES * GH * GW * FI
 
 
 def tile_graphconvlayer_t_kernel(tc, X, Wm, b, H, W, out):
     nc = tc.nc
     assert (H, W) == (GH, GW)
-    x_views = [X[i].rearrange("(a e c) f -> a e c f", e=2, c=GW) for i in range(IMAGES)]
-    out_views = [out[i].rearrange("(a e c) o -> a e c o", e=2, c=GW) for i in range(IMAGES)]
+    x_view = X.rearrange("i (r c) f -> (i r) c f", c=GW)
+    out_view = out.rearrange("i (r c) o -> (i r) c o", c=GW)
 
     with ExitStack() as ctx:
         const = ctx.enter_context(tc.tile_pool(name="const", bufs=1))
         sums = ctx.enter_context(tc.tile_pool(name="sums", bufs=3))
         quant = ctx.enter_context(tc.tile_pool(name="quant", bufs=3))
-        group = ctx.enter_context(tc.tile_pool(name="group", bufs=3))
-        outs = ctx.enter_context(tc.tile_pool(name="outs", bufs=3))
+        outs = ctx.enter_context(tc.tile_pool(name="outs", bufs=4))
         psum_ax = ctx.enter_context(tc.psum_pool(name="psum_ax", bufs=4))
         psum_o = ctx.enter_context(tc.psum_pool(name="psum_o", bufs=3))
         psum_j = ctx.enter_context(tc.psum_pool(name="psum_j", bufs=1))
         ctx.enter_context(tc.manual_schedule())
 
-        def block(q):
-            return slice(q * PAIRS, (q + 1) * PAIRS)
+        def flat(ap):
+            return ap.rearrange("p c f -> p (c f)")
 
-        xs = const.tile([P, HALF + 2, 2, FI], BF16, name="xs")
-        cuts = [0, 3, 6] + list(range(10, HALF + 3, 4))
+        xs = const.tile([P, GW + 2, FI], BF16, name="xs")
+        cuts = [0, 2, 4] + list(range(8, GW + 1, 4))
         for lo, hi in zip(cuts[:-1], cuts[1:]):
-            for q in (0, 2, 1, 3):
-                i, h = divmod(q, 2)
-                a, z = max(lo, 1 - h), min(hi, HALF + 2 - h)
-                first = HALF * h - 1
-                for e in range(2):
-                    nc.sync.dma_start(out=xs[block(q), a:z, e, :], in_=x_views[i][:, e, first + a : first + z, :])
+            nc.sync.dma_start(out=xs[:, 1 + lo : 1 + hi, :], in_=x_view[:, lo:hi, :])
         wraw = const.tile([P, PASSES * PACK, FO], BF16, name="wraw")
         nc.scalar.dma_start(out=wraw[:], in_=Wm.rearrange("(a p) n -> p a n", p=P))
         braw = const.tile([P, FO], BF16, name="braw")
         nc.scalar.dma_start(out=braw[:], in_=b.partition_broadcast(P))
 
-        fill = const.tile([P, FO * PACK], BF16, name="fill", align_bytes=64)
+        fill = const.tile([P, NPAD * PACK], BF16, name="fill", align_bytes=64)
         nc.vector.memset(fill[:], 1.0)
-        wq = const.tile([P, PASSES, NPAD], U32, name="wq", align_bytes=64)
-        wqs = const.tile([P, PASSES, NPAD], U8, name="wqs", align_bytes=64)
-        for g in reversed(range(PASSES)):
-            for lo in range(0, NPAD, FO):
-                nc.vector.quantize_mx(
-                    out=wq[:, g, lo : lo + FO].bitcast(FP8X4), scales=wqs[:, g, lo : lo + FO], in_=fill[:]
-                )
+        dq = const.tile([P, NPAD], U32, name="dq", align_bytes=64)
+        dqs = const.tile([P, NPAD], U8, name="dqs", align_bytes=64)
+        nc.vector.quantize_mx(out=dq[:].bitcast(FP8X4), scales=dqs[:], in_=fill[:])
         junk = psum_j.tile([P, NPAD], F32, name="junk")
 
         def filler_pass():
             nc.tensor.matmul_mx(
-                out=junk[:], lhsT=wq[:, 1, NPAD - P : NPAD].bitcast(FP8X4), lhsT_scale=wqs[:, 1, NPAD - P : NPAD],
-                rhs=wq[:, 1, :].bitcast(FP8X4), rhs_scale=wqs[:, 1, :], start=True, stop=True,
+                out=junk[:], lhsT=dq[:, 0:P].bitcast(FP8X4), lhsT_scale=dqs[:, 0:P],
+                rhs=dq[:].bitcast(FP8X4), rhs_scale=dqs[:], start=True, stop=True,
             )
 
         ident = const.tile([P, P], F32, name="ident")
         make_identity(nc, ident[:])
-        above = const.tile([P, P], F32, name="above")
-        below = const.tile([P, P], F32, name="below")
+        pair_a = const.tile([P, P], F32, name="pair_a")
+        pair_b = const.tile([P, P], F32, name="pair_b")
 
-        def blocks(ap):
-            return ap.rearrange("p (q a) -> p q a", q=BLOCKS)
+        def halves(ap):
+            view = ap.rearrange("p (j two) -> p j two", two=2)
+            return view[:, :, 0], view[:, :, 1]
 
-        nc.vector.memset(above[:], 0.0)
-        nc.vector.memset(below[:], 0.0)
-        for q in range(BLOCKS):
-            nc.vector.memset(xs[block(q), (HALF + 1) * (q % 2), :, :], 0.0)
-        nc.vector.tensor_copy(out=blocks(above[:])[:, :, 1:PAIRS], in_=blocks(ident[:])[:, :, 0 : PAIRS - 1])
-        nc.vector.tensor_copy(out=blocks(below[:])[:, :, 0 : PAIRS - 1], in_=blocks(ident[:])[:, :, 1:PAIRS])
-        shift = (above, below)
+        nc.vector.memset(pair_b[:], 0.0)
+        nc.vector.memset(xs[:, 0, :], 0.0)
+        nc.vector.memset(xs[:, GW + 1, :], 0.0)
+        a_even, a_odd = halves(pair_a[:])
+        i_even, i_odd = halves(ident[:])
+        nc.vector.tensor_copy(out=a_even, in_=i_odd)
+        nc.vector.tensor_copy(out=a_odd, in_=i_even)
+        for i in range(IMAGES):
+            inner = slice(i * GH + 1, i * GH + GH - 1)
+            b_first, b_second = halves(pair_b[:, inner])
+            i_first, i_second = halves(ident[:, inner])
+            nc.vector.tensor_copy(out=b_first, in_=i_second)
+            nc.vector.tensor_copy(out=b_second, in_=i_first)
+
+        band2 = const.tile([P, P], BF16, name="band2")
+        band3 = const.tile([P, P], BF16, name="band3")
+        nc.vector.tensor_tensor(out=band2[:], in0=pair_a[:], in1=pair_b[:], op=ADD)
+        nc.vector.tensor_tensor(out=band3[:], in0=band2[:], in1=ident[:], op=ADD)
+
+        wq = const.tile([P, PASSES, NPAD], U32, name="wq", align_bytes=64)
+        wqs = const.tile([P, PASSES, NPAD], U8, name="wqs", align_bytes=64)
+        for g in range(PASSES):
+            nc.vector.quantize_mx(out=wq[:, g, :].bitcast(FP8X4), scales=wqs[:, g, :], in_=fill[:])
         bias32 = const.tile([P, FO], F32, name="bias32")
 
         def prepare_weights():
@@ -108,58 +112,58 @@ def tile_graphconvlayer_t_kernel(tc, X, Wm, b, H, W, out):
         sums_of, grouped_of, codes_of, staged_of, po_of = {}, {}, {}, {}, {}
 
         def column_sums(k):
-            tt = sums.tile([P, 2, FI], F32, name="tt")
-            ss = sums.tile([P, 2, FI], F32, name="ss")
-            yy = sums.tile([P, 2, NY * P], F32, name="yy")
-            sums_of[k] = (tt, ss, yy)
-
-            def sides(rows):
-                nc.vector.tensor_tensor(out=tt[:, rows, :], in0=xs[:, k, rows, :], in1=xs[:, k + 2, rows, :], op=ADD)
-
-            def triple(rows):
-                nc.vector.tensor_tensor(out=ss[:, rows, :], in0=tt[:, rows, :], in1=xs[:, k + 1, rows, :], op=ADD)
-
-            def in_pair(e):
+            tt = sums.tile([P, CW, FI], F32, name="tt")
+            ss = sums.tile([P, CW, FI], F32, name="ss")
+            sums_of[k] = (tt, ss)
+            c0 = k * CW
+            for lo, hi in ([(0, 1), (1, 2)] if k == 1 else [(0, CW)]):
                 nc.vector.tensor_tensor(
-                    out=yy[:, e, :], in0=tt[:, e, 0 : NY * P], in1=ss[:, 1 - e, 0 : NY * P], op=ADD
+                    out=flat(tt[:, lo:hi, :]), in0=flat(xs[:, c0 + lo : c0 + hi, :]),
+                    in1=flat(xs[:, c0 + lo + 2 : c0 + hi + 2, :]), op=ADD,
+                )
+                nc.vector.tensor_tensor(
+                    out=flat(ss[:, lo:hi, :]), in0=flat(tt[:, lo:hi, :]),
+                    in1=flat(xs[:, c0 + lo + 1 : c0 + hi + 1, :]), op=ADD,
                 )
 
-            if k == 0:
-                sides(slice(1, 2))
-                triple(slice(1, 2))
-                sides(slice(0, 1))
-                in_pair(0)
-                triple(slice(0, 1))
-                in_pair(1)
-            else:
-                sides(slice(0, 2))
-                triple(slice(0, 2))
-                in_pair(0)
-                in_pair(1)
+        state = {"groups": 0, "next_col": 0, "allowed": 0, "finished": 0}
 
-        def row_sums(k, e, g):
-            tt, ss, yy = sums_of[k]
-            if (e, g) == (0, 0):
-                grouped_of[k] = group.tile([P, 2, PASSES, P, PACK], BF16, name="grouped", align_bytes=64)
+        def bunch():
+            col = state["next_col"]
+            if col < state["allowed"]:
+                for g in range(PASSES):
+                    mx_pass(col // CW, col % CW, g, NPAD)
+                state["next_col"] = col + 1
+            else:
+                for g in range(PASSES):
+                    filler_pass()
+
+        def row_sums(k, cc, g):
+            if (cc, g) == (0, 0):
+                grouped_of[k] = quant.tile([P, CW, PASSES, P, PACK], BF16, name="grouped", align_bytes=64)
             ax = psum_ax.tile([P, PACK, P], F32, name="ax")
             for t in range(PACK):
-                tile_no = g * PACK + t
-                cols = slice(tile_no * P, (tile_no + 1) * P)
-                terms = [(ss[:, 1 - e, cols], shift[e])]
-                if tile_no < NY:
-                    terms += [(yy[:, e, cols], ident)]
+                cols = slice((g * PACK + t) * P, (g * PACK + t + 1) * P)
+                if k == 0:
+                    terms = [(xs[:, cc + 2, cols], band3), (xs[:, cc + 1, cols], band2)]
+                    if cc > 0:
+                        terms = [(xs[:, cc, cols], band3)] + terms
                 else:
-                    terms += [(tt[:, e, cols], ident), (ss[:, 1 - e, cols], ident)]
+                    tt, ss = sums_of[k]
+                    terms = [(ss[:, cc, cols], pair_b), (tt[:, cc, cols], ident), (ss[:, cc, cols], pair_a)]
                 for j, (data, matrix) in enumerate(terms):
                     nc.tensor.matmul(
                         out=ax[:, t, :], lhsT=data, rhs=matrix[:],
-                        is_transpose=True, start=(j == 0), stop=(j == len(terms) - 1),
+                        is_transpose=(k > 0), start=(j == 0), stop=(j == len(terms) - 1),
                     )
-            nc.scalar.copy(out=grouped_of[k][:, e, g], in_=ax[:].rearrange("p t n -> p n t"))
+                state["groups"] += 1
+                if state["groups"] % RUN == 0:
+                    bunch()
+            nc.scalar.copy(out=grouped_of[k][:, cc, g], in_=ax[:].rearrange("p t n -> p n t"))
 
         def quantise(k):
-            codes = quant.tile([P, 2, PASSES, P], U32, name="codes", align_bytes=64)
-            scales = quant.tile([P, 2, PASSES, P], U8, name="scales", align_bytes=64)
+            codes = quant.tile([P, CW, PASSES, P], U32, name="codes", align_bytes=64)
+            scales = quant.tile([P, CW, PASSES, P], U8, name="scales", align_bytes=64)
             codes_of[k] = (codes, scales)
             nc.vector.quantize_mx(
                 out=codes[:].rearrange("p c g n -> p (c g n)").bitcast(FP8X4),
@@ -167,55 +171,56 @@ def tile_graphconvlayer_t_kernel(tc, X, Wm, b, H, W, out):
                 in_=grouped_of[k][:].rearrange("p c g n t -> p (c g n t)"),
             )
 
-        def mx_pass(k, e, g, width):
+        def mx_pass(k, cc, g, width):
             codes, scales = codes_of[k]
-            if (k % KB, e, g) == (0, 0, 0):
-                staged_of[k // KB] = outs.tile([P, 2, KB, FO], F32, name="staged")
+            if (cc, g) == (0, 0):
+                staged_of[k] = outs.tile([P, CW, FO], F32, name="staged")
             if g == 0:
                 po_of[k] = psum_o.tile([P, NPAD], F32, name="po")
             po = po_of[k]
             nc.tensor.matmul_mx(
                 out=po[:, 0:width],
-                lhsT=codes[:, e, g, :].bitcast(FP8X4),
-                lhsT_scale=scales[:, e, g, :],
+                lhsT=codes[:, cc, g, :].bitcast(FP8X4),
+                lhsT_scale=scales[:, cc, g, :],
                 rhs=wq[:, g, 0:width].bitcast(FP8X4),
                 rhs_scale=wqs[:, g, 0:width],
                 start=(g == 0),
                 stop=(g == PASSES - 1),
             )
             if g == PASSES - 1:
-                nc.scalar.copy(out=staged_of[k // KB][:, e, k % KB, :], in_=po[:, 0:FO])
+                nc.scalar.copy(out=staged_of[k][:, cc, :], in_=po[:, 0:FO])
 
-        def finish(batch):
-            staged = staged_of[batch]
-            rows = staged[:].rearrange("p e k o -> p (e k) o")
+        def finish(k):
+            staged = staged_of[k]
             nc.vector.tensor_tensor(
-                out=rows, in0=rows, in1=bias32[:].unsqueeze(1).to_broadcast([P, 2 * KB, FO]), op=ADD
+                out=staged[:], in0=staged[:], in1=bias32[:].unsqueeze(1).to_broadcast([P, CW, FO]), op=ADD
             )
-            for q in range(BLOCKS):
-                i, h = divmod(q, 2)
-                first = HALF * h + batch * KB
-                nc.sync.dma_start(out=out_views[i][:, :, first : first + KB, :], in_=staged[block(q)])
+            nc.sync.dma_start(out=out_view[:, k * CW : (k + 1) * CW, :], in_=staged[:])
 
         for n in range(FIRST_KICK):
             filler_pass()
 
-        for j in range(NCH + LAG_B):
-            if j < NCH:
+        served = []
+        for j in range(NCH + LAG_M + 2):
+            if 1 <= j < NCH:
                 column_sums(j)
             if j == 2:
                 prepare_weights()
             if 0 <= j - LAG_Q < NCH:
                 quantise(j - LAG_Q)
-            if 0 <= j - LAG_B < NCH and (j - LAG_B) % KB == KB - 1:
-                finish((j - LAG_B) // KB)
-            kt, km = j - LAG_T, j - LAG_M
-            for e in range(2):
-                for g in range(PASSES):
-                    if 0 <= kt < NCH:
-                        row_sums(kt, e, g)
-                for g in range(PASSES):
-                    if 0 <= km < NCH:
-                        mx_pass(km, e, g, NPAD if 0 <= kt < NCH else FO)
-                    elif km < 0 <= kt:
-                        filler_pass()
+            for k in range(state["finished"], served[j - 2] if j >= 2 else 0):
+                finish(k)
+                state["finished"] = k + 1
+            state["allowed"] = CW * max(0, min(NCH, j - LAG_M + 1))
+            kt = j - LAG_T
+            if 0 <= kt < NCH:
+                for cc in range(CW):
+                    for g in range(PASSES):
+                        row_sums(kt, cc, g)
+            elif kt >= NCH:
+                for col in range(state["next_col"], state["allowed"]):
+                    for g in range(PASSES):
+                        mx_pass(col // CW, col % CW, g, FO)
+                    state["next_col"] = col + 1
+            served.append(state["next_col"] // CW)
+        assert state["finished"] == NCH

@@ -19,7 +19,7 @@ NCH = GW // CW
 NPAD = 512
 LAG_T, LAG_Q, LAG_M = 1, 3, 4
 FIRST_KICK = 4
-RUN = 7
+RUN = 16
 FLOPS = 2 * IMAGES * GH * GW * FI * FO + 7 * IMAGES * GH * GW * FI
 
 
@@ -129,14 +129,15 @@ def tile_graphconvlayer_t_kernel(tc, X, Wm, b, H, W, out):
         state = {"groups": 0, "next_col": 0, "allowed": 0, "finished": 0}
 
         def bunch():
-            col = state["next_col"]
-            if col < state["allowed"]:
-                for g in range(PASSES):
-                    mx_pass(col // CW, col % CW, g, NPAD)
-                state["next_col"] = col + 1
-            else:
-                for g in range(PASSES):
-                    filler_pass()
+            for width in (NPAD, FO):
+                col = state["next_col"]
+                if col < state["allowed"]:
+                    for g in range(PASSES):
+                        mx_pass(col // CW, col % CW, g, width)
+                    state["next_col"] = col + 1
+                elif width == NPAD:
+                    for g in range(PASSES):
+                        filler_pass()
 
         def row_sums(k, cc, g):
             if (cc, g) == (0, 0):
@@ -157,9 +158,9 @@ def tile_graphconvlayer_t_kernel(tc, X, Wm, b, H, W, out):
                         is_transpose=(k > 0), start=(j == 0), stop=(j == len(terms) - 1),
                     )
                 state["groups"] += 1
-                if state["groups"] % RUN == 0:
-                    bunch()
             nc.scalar.copy(out=grouped_of[k][:, cc, g], in_=ax[:].rearrange("p t n -> p n t"))
+            if state["groups"] % RUN == 0:
+                bunch()
 
         def quantise(k):
             codes = quant.tile([P, CW, PASSES, P], U32, name="codes", align_bytes=64)

@@ -139,26 +139,32 @@ def tile_graphconvlayer_t_kernel(tc, X, Wm, b, H, W, out):
                     for g in range(PASSES):
                         filler_pass()
 
-        def row_sums(k, cc, g):
-            if (cc, g) == (0, 0):
+        def terms_of(k, cc, cols):
+            if k == 0:
+                terms = [(xs[:, cc + 2, cols], band3), (xs[:, cc + 1, cols], band2)]
+                if cc > 0:
+                    terms = [(xs[:, cc, cols], band3)] + terms
+                return terms
+            tt, ss = sums_of[k]
+            return [(ss[:, cc, cols], pair_b), (tt[:, cc, cols], ident), (ss[:, cc, cols], pair_a)]
+
+        def row_sums(k, cc):
+            if cc == 0:
                 grouped_of[k] = quant.tile([P, CW, PASSES, P, PACK], BF16, name="grouped", align_bytes=64)
-            ax = psum_ax.tile([P, PACK, P], F32, name="ax")
+            banks = [psum_ax.tile([P, PACK, P], F32, name="ax") for g in range(PASSES)]
             for t in range(PACK):
-                cols = slice((g * PACK + t) * P, (g * PACK + t + 1) * P)
-                if k == 0:
-                    terms = [(xs[:, cc + 2, cols], band3), (xs[:, cc + 1, cols], band2)]
-                    if cc > 0:
-                        terms = [(xs[:, cc, cols], band3)] + terms
-                else:
-                    tt, ss = sums_of[k]
-                    terms = [(ss[:, cc, cols], pair_b), (tt[:, cc, cols], ident), (ss[:, cc, cols], pair_a)]
-                for j, (data, matrix) in enumerate(terms):
-                    nc.tensor.matmul(
-                        out=ax[:, t, :], lhsT=data, rhs=matrix[:],
-                        is_transpose=(k > 0), start=(j == 0), stop=(j == len(terms) - 1),
-                    )
-                state["groups"] += 1
-            nc.scalar.copy(out=grouped_of[k][:, cc, g], in_=ax[:].rearrange("p t n -> p n t"))
+                terms = [terms_of(k, cc, slice((g * PACK + t) * P, (g * PACK + t + 1) * P)) for g in range(PASSES)]
+                last = len(terms[0]) - 1
+                for j in range(last + 1):
+                    for g in range(PASSES):
+                        data, matrix = terms[g][j]
+                        nc.tensor.matmul(
+                            out=banks[g][:, t, :], lhsT=data, rhs=matrix[:],
+                            is_transpose=(k > 0), start=(j == 0), stop=(j == last),
+                        )
+                state["groups"] += PASSES
+            for g in range(PASSES):
+                nc.scalar.copy(out=grouped_of[k][:, cc, g], in_=banks[g][:].rearrange("p t n -> p n t"))
             if state["groups"] % RUN == 0:
                 bunch()
 
@@ -216,8 +222,7 @@ def tile_graphconvlayer_t_kernel(tc, X, Wm, b, H, W, out):
             kt = j - LAG_T
             if 0 <= kt < NCH:
                 for cc in range(CW):
-                    for g in range(PASSES):
-                        row_sums(kt, cc, g)
+                    row_sums(kt, cc)
             elif kt >= NCH:
                 for col in range(state["next_col"], state["allowed"]):
                     for g in range(PASSES):

@@ -20,6 +20,7 @@ NPAD = 512
 LAG_T, LAG_Q, LAG_M = 1, 3, 4
 FIRST_KICK = 4
 RUN = 16
+NB = 1
 FLOPS = 2 * IMAGES * GH * GW * FI * FO + 7 * IMAGES * GH * GW * FI
 
 
@@ -87,6 +88,15 @@ def tile_graphconvlayer_t_kernel(tc, X, Wm, b, H, W, out):
             nc.vector.tensor_copy(out=b_first, in_=i_second)
             nc.vector.tensor_copy(out=b_second, in_=i_first)
 
+        inner_rows = const.tile([P, 1], F32, name="inner_rows")
+        nc.vector.reduce_sum(out=inner_rows[:], in_=pair_b[:], axis=mybir.AxisListType.X)
+        pair_c = const.tile([P, P], F32, name="pair_c")
+        nc.vector.tensor_copy(out=pair_c[:], in_=pair_b[:])
+        for i in range(IMAGES):
+            top, bottom = i * GH, i * GH + GH - 1
+            nc.vector.tensor_copy(out=pair_c[:, top : top + 1], in_=ident[:, bottom : bottom + 1])
+            nc.vector.tensor_copy(out=pair_c[:, bottom : bottom + 1], in_=ident[:, top : top + 1])
+
         band2 = const.tile([P, P], BF16, name="band2")
         band3 = const.tile([P, P], BF16, name="band3")
         nc.vector.tensor_tensor(out=band2[:], in0=pair_a[:], in1=pair_b[:], op=ADD)
@@ -114,16 +124,23 @@ def tile_graphconvlayer_t_kernel(tc, X, Wm, b, H, W, out):
         def column_sums(k):
             tt = sums.tile([P, CW, FI], F32, name="tt")
             ss = sums.tile([P, CW, FI], F32, name="ss")
-            sums_of[k] = (tt, ss)
+            xc = sums.tile([P, CW, 2, NB * P], F32, name="xc")
+            sums_of[k] = (tt, ss, xc)
             c0 = k * CW
-            for lo, hi in ([(0, 1), (1, 2)] if k == 1 else [(0, CW)]):
+            centre = xs[:, c0 + 1 : c0 + 1 + CW, 0 : NB * P]
+            nc.scalar.copy(out=xc[:, :, 0, :], in_=centre)
+            nc.scalar.activation(
+                out=xc[:, :, 1, :], in_=centre, func=mybir.ActivationFunctionType.Copy, scale=inner_rows[:, 0:1]
+            )
+            rest = slice(NB * P, FI)
+            for lo, hi in ([(0, 1), (1, 2)] if k in (1, NCH - 1) else [(0, CW)]):
                 nc.vector.tensor_tensor(
                     out=flat(tt[:, lo:hi, :]), in0=flat(xs[:, c0 + lo : c0 + hi, :]),
                     in1=flat(xs[:, c0 + lo + 2 : c0 + hi + 2, :]), op=ADD,
                 )
                 nc.vector.tensor_tensor(
-                    out=flat(ss[:, lo:hi, :]), in0=flat(tt[:, lo:hi, :]),
-                    in1=flat(xs[:, c0 + lo + 1 : c0 + hi + 1, :]), op=ADD,
+                    out=ss[:, lo:hi, rest], in0=tt[:, lo:hi, rest],
+                    in1=xs[:, c0 + lo + 1 : c0 + hi + 1, rest], op=ADD,
                 )
 
         state = {"groups": 0, "next_col": 0, "allowed": 0, "finished": 0}
@@ -139,13 +156,19 @@ def tile_graphconvlayer_t_kernel(tc, X, Wm, b, H, W, out):
                     for g in range(PASSES):
                         filler_pass()
 
-        def terms_of(k, cc, cols):
+        def terms_of(k, cc, tile_no):
+            cols = slice(tile_no * P, (tile_no + 1) * P)
             if k == 0:
                 terms = [(xs[:, cc + 2, cols], band3), (xs[:, cc + 1, cols], band2)]
                 if cc > 0:
                     terms = [(xs[:, cc, cols], band3)] + terms
                 return terms
-            tt, ss = sums_of[k]
+            tt, ss, xc = sums_of[k]
+            if tile_no < NB:
+                return [
+                    (tt[:, cc, cols], pair_b), (tt[:, cc, cols], ident), (tt[:, cc, cols], pair_a),
+                    (xc[:, cc, 0, cols], pair_a), (xc[:, cc, 1, cols], pair_c),
+                ]
             return [(ss[:, cc, cols], pair_b), (tt[:, cc, cols], ident), (ss[:, cc, cols], pair_a)]
 
         def row_sums(k, cc):
@@ -153,15 +176,15 @@ def tile_graphconvlayer_t_kernel(tc, X, Wm, b, H, W, out):
                 grouped_of[k] = quant.tile([P, CW, PASSES, P, PACK], BF16, name="grouped", align_bytes=64)
             banks = [psum_ax.tile([P, PACK, P], F32, name="ax") for g in range(PASSES)]
             for t in range(PACK):
-                terms = [terms_of(k, cc, slice((g * PACK + t) * P, (g * PACK + t + 1) * P)) for g in range(PASSES)]
-                last = len(terms[0]) - 1
-                for j in range(last + 1):
+                terms = [terms_of(k, cc, g * PACK + t) for g in range(PASSES)]
+                for j in range(max(len(terms[g]) for g in range(PASSES))):
                     for g in range(PASSES):
-                        data, matrix = terms[g][j]
-                        nc.tensor.matmul(
-                            out=banks[g][:, t, :], lhsT=data, rhs=matrix[:],
-                            is_transpose=(k > 0), start=(j == 0), stop=(j == last),
-                        )
+                        if j < len(terms[g]):
+                            data, matrix = terms[g][j]
+                            nc.tensor.matmul(
+                                out=banks[g][:, t, :], lhsT=data, rhs=matrix[:],
+                                is_transpose=(k > 0), start=(j == 0), stop=(j == len(terms[g]) - 1),
+                            )
                 state["groups"] += PASSES
             for g in range(PASSES):
                 nc.scalar.copy(out=grouped_of[k][:, cc, g], in_=banks[g][:].rearrange("p t n -> p n t"))

from contextlib import ExitStack

import concourse.mybir as mybir
from concourse.masks import make_identity

F32 = mybir.dt.float32
BF16 = mybir.dt.bfloat16
U32 = mybir.dt.uint32
U8 = mybir.dt.uint8
FP8X4 = mybir.dt.float8_e4m3fn_x4
ADD = mybir.AluOpType.add

P = 128
IMAGES, GH, GW, FI, FO = 2, 64, 64, 1024, 128
PACK = 4
PASSES = FI // (P * PACK)
CW = 2
NCH = GW // CW
NPAD = 512
LAG_T, LAG_Q, LAG_M = 1, 3, 4
FIRST_KICK = 4
RUN = 16
NB = 1
FLOPS = 2 * IMAGES * GH * GW * FI * FO + 7 * IMAGES * GH * GW * FI


def tile_graphconvlayer_t_kernel(tc, X, Wm, b, H, W, out):
    nc = tc.nc
    assert (H, W) == (GH, GW)
    x_view = X.rearrange("i (r c) f -> (i r) c f", c=GW)
    out_view = out.rearrange("i (r c) o -> (i r) c o", c=GW)

    with ExitStack() as ctx:
        const = ctx.enter_context(tc.tile_pool(name="const", bufs=1))
        sums = ctx.enter_context(tc.tile_pool(name="sums", bufs=3))
        quant = ctx.enter_context(tc.tile_pool(name="quant", bufs=3))
        outs = ctx.enter_context(tc.tile_pool(name="outs", bufs=4))
        psum_ax = ctx.enter_context(tc.psum_pool(name="psum_ax", bufs=4))
        psum_o = ctx.enter_context(tc.psum_pool(name="psum_o", bufs=3))
        psum_j = ctx.enter_context(tc.psum_pool(name="psum_j", bufs=1))
        ctx.enter_context(tc.manual_schedule())

        def flat(ap):
            return ap.rearrange("p c f -> p (c f)")

        xs = const.tile([P, GW + 2, FI], BF16, name="xs")
        cuts = [0, 2, 4] + list(range(8, GW + 1, 4))
        for lo, hi in zip(cuts[:-1], cuts[1:]):
            nc.sync.dma_start(out=xs[:, 1 + lo : 1 + hi, :], in_=x_view[:, lo:hi, :])
        wraw = const.tile([P, PASSES * PACK, FO], BF16, name="wraw")
        nc.scalar.dma_start(out=wraw[:], in_=Wm.rearrange("(a p) n -> p a n", p=P))
        braw = const.tile([P, FO], BF16, name="braw")
        nc.scalar.dma_start(out=braw[:], in_=b.partition_broadcast(P))

        fill = const.tile([P, NPAD * PACK], BF16, name="fill", align_bytes=64)
        nc.vector.memset(fill[:], 1.0)
        dq = const.tile([P, NPAD], U32, name="dq", align_bytes=64)
        dqs = const.tile([P, NPAD], U8, name="dqs", align_bytes=64)
        nc.vector.quantize_mx(out=dq[:].bitcast(FP8X4), scales=dqs[:], in_=fill[:])
        junk = psum_j.tile([P, NPAD], F32, name="junk")

        def filler_pass():
            nc.tensor.matmul_mx(
                out=junk[:], lhsT=dq[:, 0:P].bitcast(FP8X4), lhsT_scale=dqs[:, 0:P],
                rhs=dq[:].bitcast(FP8X4), rhs_scale=dqs[:], start=True, stop=True,
            )

        ident = const.tile([P, P], F32, name="ident")
        make_identity(nc, ident[:])
        pair_a = const.tile([P, P], F32, name="pair_a")
        pair_b = const.tile([P, P], F32, name="pair_b")

        def halves(ap):
            view = ap.rearrange("p (j two) -> p j two", two=2)
            return view[:, :, 0], view[:, :, 1]

        nc.vector.memset(pair_b[:], 0.0)
        nc.vector.memset(xs[:, 0, :], 0.0)
        nc.vector.memset(xs[:, GW + 1, :], 0.0)
        a_even, a_odd = halves(pair_a[:])
        i_even, i_odd = halves(ident[:])
        nc.vector.tensor_copy(out=a_even, in_=i_odd)
        nc.vector.tensor_copy(out=a_odd, in_=i_even)
        for i in range(IMAGES):
            inner = slice(i * GH + 1, i * GH + GH - 1)
            b_first, b_second = halves(pair_b[:, inner])
            i_first, i_second = halves(ident[:, inner])
            nc.vector.tensor_copy(out=b_first, in_=i_second)
            nc.vector.tensor_copy(out=b_second, in_=i_first)

        inner_rows = const.tile([P, 1], F32, name="inner_rows")
        nc.vector.reduce_sum(out=inner_rows[:], in_=pair_b[:], axis=mybir.AxisListType.X)
        pair_c = const.tile([P, P], F32, name="pair_c")
        nc.vector.tensor_copy(out=pair_c[:], in_=pair_b[:])
        for i in range(IMAGES):
            top, bottom = i * GH, i * GH + GH - 1
            nc.vector.tensor_copy(out=pair_c[:, top : top + 1], in_=ident[:, bottom : bottom + 1])
            nc.vector.tensor_copy(out=pair_c[:, bottom : bottom + 1], in_=ident[:, top : top + 1])

        band2 = const.tile([P, P], BF16, name="band2")
        band3 = const.tile([P, P], BF16, name="band3")
        nc.vector.tensor_tensor(out=band2[:], in0=pair_a[:], in1=pair_b[:], op=ADD)
        nc.vector.tensor_tensor(out=band3[:], in0=band2[:], in1=ident[:], op=ADD)

        wq = const.tile([P, PASSES, NPAD], U32, name="wq", align_bytes=64)
        wqs = const.tile([P, PASSES, NPAD], U8, name="wqs", align_bytes=64)
        for g in range(PASSES):
            nc.vector.quantize_mx(out=wq[:, g, :].bitcast(FP8X4), scales=wqs[:, g, :], in_=fill[:])
        bias32 = const.tile([P, FO], F32, name="bias32")

        def prepare_weights():
            wgrp = const.tile([P, PASSES, FO, PACK], BF16, name="wgrp", align_bytes=64)
            nc.vector.tensor_copy(out=wgrp[:], in_=wraw[:].rearrange("p (g t) n -> p g n t", t=PACK))
            nc.vector.tensor_copy(out=bias32[:], in_=braw[:])
            for g in range(PASSES):
                nc.vector.quantize_mx(
                    out=wq[:, g, 0:FO].bitcast(FP8X4),
                    scales=wqs[:, g, 0:FO],
                    in_=wgrp[:, g].rearrange("p n t -> p (n t)"),
                )

        sums_of, grouped_of, codes_of, staged_of, po_of = {}, {}, {}, {}, {}

        def column_sums(k):
            tt = sums.tile([P, CW, FI], F32, name="tt")
            ss = sums.tile([P, CW, FI], F32, name="ss")
            xc = sums.tile([P, CW, 2, NB * P], F32, name="xc")
            sums_of[k] = (tt, ss, xc)
            c0 = k * CW
            centre = xs[:, c0 + 1 : c0 + 1 + CW, 0 : NB * P]
            nc.scalar.copy(out=xc[:, :, 0, :], in_=centre)
            nc.scalar.activation(
                out=xc[:, :, 1, :], in_=centre, func=mybir.ActivationFunctionType.Copy, scale=inner_rows[:, 0:1]
            )
            rest = slice(NB * P, FI)
            for lo, hi in ([(0, 1), (1, 2)] if k in (1, NCH - 1) else [(0, CW)]):
                nc.vector.tensor_tensor(
                    out=flat(tt[:, lo:hi, :]), in0=flat(xs[:, c0 + lo : c0 + hi, :]),
                    in1=flat(xs[:, c0 + lo + 2 : c0 + hi + 2, :]), op=ADD,
                )
                nc.vector.tensor_tensor(
                    out=ss[:, lo:hi, rest], in0=tt[:, lo:hi, rest],
                    in1=xs[:, c0 + lo + 1 : c0 + hi + 1, rest], op=ADD,
                )

        state = {"groups": 0, "next_col": 0, "allowed": 0, "finished": 0}

        def bunch():
            for width in (NPAD, FO):
                col = state["next_col"]
                if col < state["allowed"]:
                    for g in range(PASSES):
                        mx_pass(col // CW, col % CW, g, width)
                    state["next_col"] = col + 1
                elif width == NPAD:
                    for g in range(PASSES):
                        filler_pass()

        def terms_of(k, cc, tile_no):
            cols = slice(tile_no * P, (tile_no + 1) * P)
            if k == 0:
                terms = [(xs[:, cc + 2, cols], band3), (xs[:, cc + 1, cols], band2)]
                if cc > 0:
                    terms = [(xs[:, cc, cols], band3)] + terms
                return terms
            tt, ss, xc = sums_of[k]
            if tile_no < NB:
                return [
                    (tt[:, cc, cols], pair_b), (tt[:, cc, cols], ident), (tt[:, cc, cols], pair_a),
                    (xc[:, cc, 0, cols], pair_a), (xc[:, cc, 1, cols], pair_c),
                ]
            return [(ss[:, cc, cols], pair_b), (tt[:, cc, cols], ident), (ss[:, cc, cols], pair_a)]

        def row_sums(k, cc):
            if cc == 0:
                grouped_of[k] = quant.tile([P, CW, PASSES, P, PACK], BF16, name="grouped", align_bytes=64)
            banks = [psum_ax.tile([P, PACK, P], F32, name="ax") for g in range(PASSES)]
            for t in range(PACK):
                terms = [terms_of(k, cc, g * PACK + t) for g in range(PASSES)]
                for j in range(max(len(terms[g]) for g in range(PASSES))):
                    for g in range(PASSES):
                        if j < len(terms[g]):
                            data, matrix = terms[g][j]
                            nc.tensor.matmul(
                                out=banks[g][:, t, :], lhsT=data, rhs=matrix[:],
                                is_transpose=(k > 0), start=(j == 0), stop=(j == len(terms[g]) - 1),
                            )
                state["groups"] += PASSES
            for g in range(PASSES):
                nc.scalar.copy(out=grouped_of[k][:, cc, g], in_=banks[g][:].rearrange("p t n -> p n t"))
            if state["groups"] % RUN == 0:
                bunch()

        def quantise(k):
            codes = quant.tile([P, CW, PASSES, P], U32, name="codes", align_bytes=64)
            scales = quant.tile([P, CW, PASSES, P], U8, name="scales", align_bytes=64)
            codes_of[k] = (codes, scales)
            nc.vector.quantize_mx(
                out=codes[:].rearrange("p c g n -> p (c g n)").bitcast(FP8X4),
                scales=scales[:].rearrange("p c g n -> p (c g n)"),
                in_=grouped_of[k][:].rearrange("p c g n t -> p (c g n t)"),
            )

        def mx_pass(k, cc, g, width):
            codes, scales = codes_of[k]
            if (cc, g) == (0, 0):
                staged_of[k] = outs.tile([P, CW, FO], F32, name="staged")
            if g == 0:
                po_of[k] = psum_o.tile([P, NPAD], F32, name="po")
            po = po_of[k]
            nc.tensor.matmul_mx(
                out=po[:, 0:width],
                lhsT=codes[:, cc, g, :].bitcast(FP8X4),
                lhsT_scale=scales[:, cc, g, :],
                rhs=wq[:, g, 0:width].bitcast(FP8X4),
                rhs_scale=wqs[:, g, 0:width],
                start=(g == 0),
                stop=(g == PASSES - 1),
            )
            if g == PASSES - 1:
                nc.scalar.copy(out=staged_of[k][:, cc, :], in_=po[:, 0:FO])

        def finish(k):
            staged = staged_of[k]
            nc.vector.tensor_tensor(
                out=staged[:], in0=staged[:], in1=bias32[:].unsqueeze(1).to_broadcast([P, CW, FO]), op=ADD
            )
            nc.sync.dma_start(out=out_view[:, k * CW : (k + 1) * CW, :], in_=staged[:])

        for n in range(FIRST_KICK):
            filler_pass()

        served = []
        for j in range(NCH + LAG_M + 2):
            if 1 <= j < NCH:
                column_sums(j)
            if j == 2:
                prepare_weights()
            if 0 <= j - LAG_Q < NCH:
                quantise(j - LAG_Q)
            for k in range(state["finished"], served[j - 2] if j >= 2 else 0):
                finish(k)
                state["finished"] = k + 1
            state["allowed"] = CW * max(0, min(NCH, j - LAG_M + 1))
            kt = j - LAG_T
            if 0 <= kt < NCH:
                for cc in range(CW):
                    row_sums(kt, cc)
            elif kt >= NCH:
                for col in range(state["next_col"], state["allowed"]):
                    for g in range(PASSES):
                        mx_pass(col // CW, col % CW, g, FO)
                    state["next_col"] = col + 1
            served.append(state["next_col"] // CW)
        assert state["finished"] == NCH
